import numpy as np
import ml_dtypes

BF16 = ml_dtypes.bfloat16


def bf(x):
    return np.asarray(x, np.float32).astype(BF16)


def f32(x):
    return np.asarray(x, np.float32)


def f64(x):
    return np.asarray(x).astype(np.float64)


def striped(idx):
    return np.tile(idx.reshape(-1, 16).T, (8, 1))


S, D, U, N, H1, H2 = 512, 128, 128, 256, 512, 128


def setup_inputs():
    return {
        "item_emb": bf(np.random.standard_normal((S, D))),
        "user_emb": bf(np.random.standard_normal((D, U))),
        "w1i": bf(np.random.standard_normal((D, H1)) / np.sqrt(2.0 * D)),
        "w1u": bf(np.random.standard_normal((D, H1)) / np.sqrt(2.0 * D)),
        "b1": f32(0.25 * np.random.standard_normal((H1, 1))),
        "w2": bf(np.random.standard_normal((H1, H2)) * np.sqrt(2.0 / H1)),
        "b2": f32(0.25 * np.random.standard_normal((H2, 1))),
        "offs": striped(np.random.permutation(S)[:N]),
    }


def reference(item_emb, user_emb, w1i, w1u, b1, w2, b2, offs):
    idx = offs[:16].T.reshape(-1)
    h = f64(item_emb)[idx].T
    w = f64(user_emb)
    pi = f64(w1i).T @ h
    pu = f64(w1u).T @ w
    h1 = np.maximum(pu[:, :, None] + pi[:, None, :] + f64(b1)[:, :, None], 0.0).reshape(H1, U * N)
    h2 = np.maximum(f64(w2).T @ h1 + f64(b2), 0.0)
    gmf = (w[:, :, None] * h[:, None, :]).reshape(D, U * N)
    return np.concatenate([gmf, h2], axis=0)

@@ -1,0 +1,119 @@
+import concourse.mybir as mybir
+from concourse.masks import make_identity
+
+BF16, F32, U16 = mybir.dt.bfloat16, mybir.dt.float32, mybir.dt.uint16
+ADD, MAX, MULT = mybir.AluOpType.add, mybir.AluOpType.max, mybir.AluOpType.mult
+RELU = mybir.ActivationFunctionType.Relu
+
+P = 128
+S, D, U, N, H1, H2 = 512, 128, 128, 256, 512, 128
+SONG_BLOCKS = S // P
+HID_BLOCKS = H1 // P
+BANK = 512
+PAIR = BANK // N
+CHUNK = 8
+SCALAR_BLOCK = HID_BLOCKS - 1
+
+FLOPS = 2 * D * H1 * (N + U) + 2 * H1 * H2 * U * N
+
+
+def tile_modelncf_b_kernel(tc, item_emb, user_emb, w1i, w1u, b1, w2, b2, offs, out):
+    nc = tc.nc
+    with tc.tile_pool(name="held", bufs=1) as held:
+        offsets = held.tile([P, N // 16], U16, name="offsets")
+        table = held.tile([P, S], BF16, name="table")
+        ident = held.tile([P, P], BF16, name="ident")
+        user_sb = held.tile([P, U], BF16, name="user_sb")
+        w2_sb = held.tile([P, HID_BLOCKS, H2], BF16, name="w2_sb")
+        bias_cols = held.tile([P, HID_BLOCKS + 1], F32, name="bias_cols")
+        pi_sb = held.tile([P, HID_BLOCKS, N], F32, name="pi_sb")
+        pub_sb = held.tile([P, HID_BLOCKS, U], F32, name="pub_sb")
+        h_sb = held.tile([P, N], F32, name="h_sb")
+
+        with (
+            tc.tile_pool(name="setup", bufs=1) as setup,
+            tc.psum_pool(name="setup_psum", bufs=1) as setup_psum,
+        ):
+            item_rows = setup.tile([P, SONG_BLOCKS, D], BF16, name="item_rows")
+            w1i_sb = setup.tile([P, H1], BF16, name="w1i_sb")
+            w1u_sb = setup.tile([P, H1], BF16, name="w1u_sb")
+            bias_rows = setup.tile([P, P], F32, name="bias_rows")
+            ident_f32 = setup.tile([P, P], F32, name="ident_f32")
+
+            nc.sync.dma_start(offsets[:], offs)
+            nc.sync.dma_start(item_rows[:], item_emb.rearrange("(k p) e -> p k e", p=P))
+            nc.sync.dma_start(w1i_sb[:], w1i)
+            nc.scalar.dma_start(user_sb[:], user_emb)
+            nc.scalar.dma_start(w1u_sb[:], w1u)
+            nc.scalar.dma_start(w2_sb[:], w2.rearrange("(k p) r -> p k r", p=P))
+            nc.vector.memset(bias_rows[:], 0.0)
+            nc.gpsimd.dma_start(bias_rows[0:HID_BLOCKS, :], b1.rearrange("(k m) o -> k (m o)", m=P))
+            nc.gpsimd.dma_start(bias_rows[HID_BLOCKS : HID_BLOCKS + 1, :], b2.rearrange("r o -> o r"))
+            make_identity(nc, ident[:])
+            make_identity(nc, ident_f32[:])
+
+            bias_ps = setup_psum.tile([P, P], F32, name="bias_ps")
+            nc.tensor.transpose(bias_ps[:], bias_rows[:], ident_f32[:])
+            nc.vector.tensor_copy(bias_cols[:], bias_ps[:, 0 : HID_BLOCKS + 1])
+
+            table_ps = setup_psum.tile([P, S], BF16, name="table_ps")
+            for k in range(SONG_BLOCKS):
+                nc.tensor.transpose(table_ps[:, k * P : (k + 1) * P], item_rows[:, k, :], ident[:])
+            nc.vector.tensor_copy(table[:], table_ps[:])
+
+            pu_ps = setup_psum.tile([P, HID_BLOCKS, U], F32, name="pu_ps")
+            for m in range(HID_BLOCKS):
+                nc.tensor.matmul(pu_ps[:, m, :], w1u_sb[:, m * P : (m + 1) * P], user_sb[:], start=True, stop=True)
+                nc.vector.tensor_scalar(pub_sb[:, m, :], pu_ps[:, m, :], bias_cols[:, m : m + 1], None, ADD)
+
+            for m in range(HID_BLOCKS):
+                pi_ps = setup_psum.tile([P, N], F32, name=f"pi_ps{m}")
+                nc.tensor.matmul(
+                    pi_ps[:], w1i_sb[:, m * P : (m + 1) * P], table[:].indirect(offsets[:]), start=True, stop=True
+                )
+                if m == SCALAR_BLOCK:
+                    nc.scalar.copy(pi_sb[:, m, :], pi_ps[:])
+                else:
+                    nc.vector.tensor_copy(pi_sb[:, m, :], pi_ps[:])
+            h_ps = setup_psum.tile([P, N], F32, name="h_ps")
+            nc.tensor.matmul(h_ps[:], ident[:], table[:].indirect(offsets[:]), start=True, stop=True)
+            nc.vector.tensor_copy(h_sb[:], h_ps[:])
+
+        with (
+            tc.tile_pool(name="hidden", bufs=4) as hidden,
+            tc.tile_pool(name="staged", bufs=3) as staged,
+            tc.psum_pool(name="acc_psum", bufs=4) as acc_psum,
+        ):
+            for first_user in range(0, U, CHUNK):
+                mlp_out = staged.tile([P, CHUNK * N], F32, name="mlp_out")
+                gmf_out = staged.tile([P, CHUNK * N], F32, name="gmf_out")
+                for pair in range(CHUNK // PAIR):
+                    h1 = hidden.tile([P, HID_BLOCKS, BANK], BF16, name="h1")
+                    for m in range(HID_BLOCKS):
+                        for t in range(PAIR):
+                            u = first_user + pair * PAIR + t
+                            h1_piece = h1[:, m, t * N : (t + 1) * N]
+                            if m == SCALAR_BLOCK:
+                                nc.scalar.activation(h1_piece, pi_sb[:, m, :], RELU, bias=pub_sb[:, m, u : u + 1])
+                            else:
+                                nc.vector.tensor_scalar(
+                                    h1_piece, pi_sb[:, m, :], pub_sb[:, m, u : u + 1], 0.0, ADD, MAX
+                                )
+                    acc = acc_psum.tile([P, BANK], F32, name="acc")
+                    for m in range(HID_BLOCKS):
+                        nc.tensor.matmul(
+                            acc[:], w2_sb[:, m, :], h1[:, m, :], start=(m == 0), stop=(m == HID_BLOCKS - 1)
+                        )
+                    nc.scalar.activation(
+                        mlp_out[:, pair * BANK : (pair + 1) * BANK],
+                        acc[:],
+                        RELU,
+                        bias=bias_cols[:, HID_BLOCKS : HID_BLOCKS + 1],
+                    )
+                    for t in range(PAIR):
+                        u = first_user + pair * PAIR + t
+                        col = (pair * PAIR + t) * N
+                        nc.vector.tensor_scalar(gmf_out[:, col : col + N], h_sb[:], user_sb[:, u : u + 1], None, MULT)
+                cols = slice(first_user * N, (first_user + CHUNK) * N)
+                nc.sync.dma_start(out[0:D, cols], gmf_out[:])
+                nc.sync.dma_start(out[D : D + H2, cols], mlp_out[:])

@@ -12,6 +12,7 @@ HID_BLOCKS = H1 // P
 BANK = 512
 PAIR = BANK // N
 CHUNK = 8
+STORE_USERS = [CHUNK] * (U // CHUNK - 1) + [4, 2, 2]
 SCALAR_BLOCK = HID_BLOCKS - 1
 
 FLOPS = 2 * D * H1 * (N + U) + 2 * H1 * H2 * U * N
@@ -40,31 +41,22 @@ def tile_modelncf_b_kernel(tc, item_emb, user_emb, w1i, w1u, b1, w2, b2, offs, o
             bias_rows = setup.tile([P, P], F32, name="bias_rows")
             ident_f32 = setup.tile([P, P], F32, name="ident_f32")
 
-            nc.sync.dma_start(offsets[:], offs)
+            nc.vector.memset(bias_rows[:], 0.0)
+            make_identity(nc, ident[:])
+            nc.vector.tensor_copy(ident_f32[:], ident[:])
             nc.sync.dma_start(item_rows[:], item_emb.rearrange("(k p) e -> p k e", p=P))
-            nc.sync.dma_start(w1i_sb[:], w1i)
+            nc.sync.dma_start(offsets[:], offs)
+            nc.sync.dma_start(bias_rows[0:HID_BLOCKS, :], b1.rearrange("(k m) o -> k (m o)", m=P))
+            nc.sync.dma_start(bias_rows[HID_BLOCKS : HID_BLOCKS + 1, :], b2.rearrange("r o -> o r"))
+            nc.sync.dma_start(w2_sb[:], w2.rearrange("(k p) r -> p k r", p=P))
+            nc.scalar.dma_start(w1i_sb[:], w1i)
             nc.scalar.dma_start(user_sb[:], user_emb)
             nc.scalar.dma_start(w1u_sb[:], w1u)
-            nc.scalar.dma_start(w2_sb[:], w2.rearrange("(k p) r -> p k r", p=P))
-            nc.vector.memset(bias_rows[:], 0.0)
-            nc.gpsimd.dma_start(bias_rows[0:HID_BLOCKS, :], b1.rearrange("(k m) o -> k (m o)", m=P))
-            nc.gpsimd.dma_start(bias_rows[HID_BLOCKS : HID_BLOCKS + 1, :], b2.rearrange("r o -> o r"))
-            make_identity(nc, ident[:])
-            make_identity(nc, ident_f32[:])
-
-            bias_ps = setup_psum.tile([P, P], F32, name="bias_ps")
-            nc.tensor.transpose(bias_ps[:], bias_rows[:], ident_f32[:])
-            nc.vector.tensor_copy(bias_cols[:], bias_ps[:, 0 : HID_BLOCKS + 1])
 
             table_ps = setup_psum.tile([P, S], BF16, name="table_ps")
             for k in range(SONG_BLOCKS):
                 nc.tensor.transpose(table_ps[:, k * P : (k + 1) * P], item_rows[:, k, :], ident[:])
             nc.vector.tensor_copy(table[:], table_ps[:])
-
-            pu_ps = setup_psum.tile([P, HID_BLOCKS, U], F32, name="pu_ps")
-            for m in range(HID_BLOCKS):
-                nc.tensor.matmul(pu_ps[:, m, :], w1u_sb[:, m * P : (m + 1) * P], user_sb[:], start=True, stop=True)
-                nc.vector.tensor_scalar(pub_sb[:, m, :], pu_ps[:, m, :], bias_cols[:, m : m + 1], None, ADD)
 
             for m in range(HID_BLOCKS):
                 pi_ps = setup_psum.tile([P, N], F32, name=f"pi_ps{m}")
@@ -79,20 +71,31 @@ def tile_modelncf_b_kernel(tc, item_emb, user_emb, w1i, w1u, b1, w2, b2, offs, o
             nc.tensor.matmul(h_ps[:], ident[:], table[:].indirect(offsets[:]), start=True, stop=True)
             nc.vector.tensor_copy(h_sb[:], h_ps[:])
 
+            bias_ps = setup_psum.tile([P, P], F32, name="bias_ps")
+            nc.tensor.transpose(bias_ps[:], bias_rows[:], ident_f32[:])
+            nc.vector.tensor_copy(bias_cols[:], bias_ps[:, 0 : HID_BLOCKS + 1])
+
+            pu_ps = setup_psum.tile([P, HID_BLOCKS, U], F32, name="pu_ps")
+            for m in range(HID_BLOCKS):
+                nc.tensor.matmul(pu_ps[:, m, :], w1u_sb[:, m * P : (m + 1) * P], user_sb[:], start=True, stop=True)
+                nc.vector.tensor_scalar(pub_sb[:, m, :], pu_ps[:, m, :], bias_cols[:, m : m + 1], None, ADD)
+
         with (
-            tc.tile_pool(name="hidden", bufs=4) as hidden,
+            tc.tile_pool(name="hidden", bufs=3) as hidden,
             tc.tile_pool(name="staged", bufs=3) as staged,
-            tc.psum_pool(name="acc_psum", bufs=4) as acc_psum,
+            tc.psum_pool(name="acc_psum", bufs=8) as acc_psum,
         ):
-            for first_user in range(0, U, CHUNK):
-                mlp_out = staged.tile([P, CHUNK * N], F32, name="mlp_out")
-                gmf_out = staged.tile([P, CHUNK * N], F32, name="gmf_out")
-                for pair in range(CHUNK // PAIR):
-                    h1 = hidden.tile([P, HID_BLOCKS, BANK], BF16, name="h1")
+            first_user = 0
+            for users in STORE_USERS:
+                mlp_out = staged.tile([P, users * N], F32, name="mlp_out")
+                gmf_out = staged.tile([P, users * N], F32, name="gmf_out")
+                h1 = hidden.tile([P, HID_BLOCKS, users * N], BF16, name="h1")
+                for pair in range(users // PAIR):
                     for m in range(HID_BLOCKS):
                         for t in range(PAIR):
                             u = first_user + pair * PAIR + t
-                            h1_piece = h1[:, m, t * N : (t + 1) * N]
+                            col = (pair * PAIR + t) * N
+                            h1_piece = h1[:, m, col : col + N]
                             if m == SCALAR_BLOCK:
                                 nc.scalar.activation(h1_piece, pi_sb[:, m, :], RELU, bias=pub_sb[:, m, u : u + 1])
                             else:
@@ -102,7 +105,11 @@ def tile_modelncf_b_kernel(tc, item_emb, user_emb, w1i, w1u, b1, w2, b2, offs, o
                     acc = acc_psum.tile([P, BANK], F32, name="acc")
                     for m in range(HID_BLOCKS):
                         nc.tensor.matmul(
-                            acc[:], w2_sb[:, m, :], h1[:, m, :], start=(m == 0), stop=(m == HID_BLOCKS - 1)
+                            acc[:],
+                            w2_sb[:, m, :],
+                            h1[:, m, pair * BANK : (pair + 1) * BANK],
+                            start=(m == 0),
+                            stop=(m == HID_BLOCKS - 1),
                         )
                     nc.scalar.activation(
                         mlp_out[:, pair * BANK : (pair + 1) * BANK],
@@ -114,6 +121,7 @@ def tile_modelncf_b_kernel(tc, item_emb, user_emb, w1i, w1u, b1, w2, b2, offs, o
                         u = first_user + pair * PAIR + t
                         col = (pair * PAIR + t) * N
                         nc.vector.tensor_scalar(gmf_out[:, col : col + N], h_sb[:], user_sb[:, u : u + 1], None, MULT)
-                cols = slice(first_user * N, (first_user + CHUNK) * N)
+                cols = slice(first_user * N, (first_user + users) * N)
                 nc.sync.dma_start(out[0:D, cols], gmf_out[:])
                 nc.sync.dma_start(out[D : D + H2, cols], mlp_out[:])
+                first_user += users

@@ -82,7 +82,7 @@ def tile_modelncf_b_kernel(tc, item_emb, user_emb, w1i, w1u, b1, w2, b2, offs, o
 
         with (
             tc.tile_pool(name="hidden", bufs=3) as hidden,
-            tc.tile_pool(name="staged", bufs=3) as staged,
+            tc.tile_pool(name="staged", bufs=6) as staged,
             tc.psum_pool(name="acc_psum", bufs=8) as acc_psum,
         ):
             first_user = 0

@@ -14,6 +14,7 @@ PAIR = BANK // N
 CHUNK = 8
 STORE_USERS = [CHUNK] * (U // CHUNK - 1) + [4, 2, 2]
 SCALAR_BLOCK = HID_BLOCKS - 1
+GPSIMD_EVERY = 4
 
 FLOPS = 2 * D * H1 * (N + U) + 2 * H1 * H2 * U * N
 
@@ -120,7 +121,14 @@ def tile_modelncf_b_kernel(tc, item_emb, user_emb, w1i, w1u, b1, w2, b2, offs, o
                     for t in range(PAIR):
                         u = first_user + pair * PAIR + t
                         col = (pair * PAIR + t) * N
-                        nc.vector.tensor_scalar(gmf_out[:, col : col + N], h_sb[:], user_sb[:, u : u + 1], None, MULT)
+                        if u % GPSIMD_EVERY == GPSIMD_EVERY - 1:
+                            nc.gpsimd.tensor_scalar(
+                                gmf_out[:, col : col + N], h_sb[:], user_sb[:, u : u + 1], 1.0, MULT, MULT
+                            )
+                        else:
+                            nc.vector.tensor_scalar(
+                                gmf_out[:, col : col + N], h_sb[:], user_sb[:, u : u + 1], None, MULT
+                            )
                 cols = slice(first_user * N, (first_user + users) * N)
                 nc.sync.dma_start(out[0:D, cols], gmf_out[:])
                 nc.sync.dma_start(out[D : D + H2, cols], mlp_out[:])

@@ -14,7 +14,8 @@ PAIR = BANK // N
 CHUNK = 8
 STORE_USERS = [CHUNK] * (U // CHUNK - 1) + [4, 2, 2]
 SCALAR_BLOCK = HID_BLOCKS - 1
-GPSIMD_EVERY = 4
+SHARED_BLOCK = HID_BLOCKS - 2
+SHARED_EVERY = 8
 
 FLOPS = 2 * D * H1 * (N + U) + 2 * H1 * H2 * U * N
 
@@ -97,7 +98,7 @@ def tile_modelncf_b_kernel(tc, item_emb, user_emb, w1i, w1u, b1, w2, b2, offs, o
                             u = first_user + pair * PAIR + t
                             col = (pair * PAIR + t) * N
                             h1_piece = h1[:, m, col : col + N]
-                            if m == SCALAR_BLOCK:
+                            if m == SCALAR_BLOCK or (m == SHARED_BLOCK and u % SHARED_EVERY == SHARED_EVERY - 1):
                                 nc.scalar.activation(h1_piece, pi_sb[:, m, :], RELU, bias=pub_sb[:, m, u : u + 1])
                             else:
                                 nc.vector.tensor_scalar(
@@ -121,14 +122,7 @@ def tile_modelncf_b_kernel(tc, item_emb, user_emb, w1i, w1u, b1, w2, b2, offs, o
                     for t in range(PAIR):
                         u = first_user + pair * PAIR + t
                         col = (pair * PAIR + t) * N
-                        if u % GPSIMD_EVERY == GPSIMD_EVERY - 1:
-                            nc.gpsimd.tensor_scalar(
-                                gmf_out[:, col : col + N], h_sb[:], user_sb[:, u : u + 1], 1.0, MULT, MULT
-                            )
-                        else:
-                            nc.vector.tensor_scalar(
-                                gmf_out[:, col : col + N], h_sb[:], user_sb[:, u : u + 1], None, MULT
-                            )
+                        nc.vector.tensor_scalar(gmf_out[:, col : col + N], h_sb[:], user_sb[:, u : u + 1], None, MULT)
                 cols = slice(first_user * N, (first_user + users) * N)
                 nc.sync.dma_start(out[0:D, cols], gmf_out[:])
                 nc.sync.dma_start(out[D : D + H2, cols], mlp_out[:])

@@ -13,9 +13,10 @@ BANK = 512
 PAIR = BANK // N
 CHUNK = 8
 STORE_USERS = [CHUNK] * (U // CHUNK - 1) + [4, 2, 2]
-SCALAR_BLOCK = HID_BLOCKS - 1
-SHARED_BLOCK = HID_BLOCKS - 2
+SCALAR_BLOCK = 0
+SHARED_BLOCK = 1
 SHARED_EVERY = 8
+WARM_MATMULS = 5
 
 FLOPS = 2 * D * H1 * (N + U) + 2 * H1 * H2 * U * N
 
@@ -42,6 +43,12 @@ def tile_modelncf_b_kernel(tc, item_emb, user_emb, w1i, w1u, b1, w2, b2, offs, o
             w1u_sb = setup.tile([P, H1], BF16, name="w1u_sb")
             bias_rows = setup.tile([P, P], F32, name="bias_rows")
             ident_f32 = setup.tile([P, P], F32, name="ident_f32")
+            zeros = setup.tile([P, BANK], BF16, name="zeros")
+            h_ps = setup_psum.tile([P, BANK], F32, name="h_ps")
+
+            nc.vector.memset(zeros[:], 0.0)
+            for i in range(WARM_MATMULS):
+                nc.tensor.matmul(h_ps[:], zeros[:, 0:P], zeros[:], start=True, stop=True)
 
             nc.vector.memset(bias_rows[:], 0.0)
             make_identity(nc, ident[:])
@@ -69,9 +76,8 @@ def tile_modelncf_b_kernel(tc, item_emb, user_emb, w1i, w1u, b1, w2, b2, offs, o
                     nc.scalar.copy(pi_sb[:, m, :], pi_ps[:])
                 else:
                     nc.vector.tensor_copy(pi_sb[:, m, :], pi_ps[:])
-            h_ps = setup_psum.tile([P, N], F32, name="h_ps")
-            nc.tensor.matmul(h_ps[:], ident[:], table[:].indirect(offsets[:]), start=True, stop=True)
-            nc.vector.tensor_copy(h_sb[:], h_ps[:])
+            nc.tensor.matmul(h_ps[:, 0:N], ident[:], table[:].indirect(offsets[:]), start=True, stop=True)
+            nc.vector.tensor_copy(h_sb[:], h_ps[:, 0:N])
 
             bias_ps = setup_psum.tile([P, P], F32, name="bias_ps")
             nc.tensor.transpose(bias_ps[:], bias_rows[:], ident_f32[:])

@@ -13,12 +13,19 @@ BANK = 512
 PAIR = BANK // N
 CHUNK = 8
 STORE_USERS = [CHUNK] * (U // CHUNK - 1) + [4, 2, 2]
-SCALAR_BLOCK = 0
-SHARED_BLOCK = 1
+SCALAR_BLOCK = HID_BLOCKS - 1
+SHARED_BLOCK = HID_BLOCKS - 2
 SHARED_EVERY = 8
-WARM_MATMULS = 5
+EVICT_LAG = 2
 
 FLOPS = 2 * D * H1 * (N + U) + 2 * H1 * H2 * U * N
+
+
+def evict_and_store(nc, out, b2_col, job):
+    acc, mlp_out, pair, users, first_user = job
+    nc.scalar.activation(mlp_out[:, pair * BANK : (pair + 1) * BANK], acc[:], RELU, bias=b2_col)
+    if pair == users // PAIR - 1:
+        nc.sync.dma_start(out[D : D + H2, first_user * N : (first_user + users) * N], mlp_out[:])
 
 
 def tile_modelncf_b_kernel(tc, item_emb, user_emb, w1i, w1u, b1, w2, b2, offs, out):
@@ -33,6 +40,7 @@ def tile_modelncf_b_kernel(tc, item_emb, user_emb, w1i, w1u, b1, w2, b2, offs, o
         pi_sb = held.tile([P, HID_BLOCKS, N], F32, name="pi_sb")
         pub_sb = held.tile([P, HID_BLOCKS, U], F32, name="pub_sb")
         h_sb = held.tile([P, N], F32, name="h_sb")
+        b2_col = bias_cols[:, HID_BLOCKS : HID_BLOCKS + 1]
 
         with (
             tc.tile_pool(name="setup", bufs=1) as setup,
@@ -43,12 +51,6 @@ def tile_modelncf_b_kernel(tc, item_emb, user_emb, w1i, w1u, b1, w2, b2, offs, o
             w1u_sb = setup.tile([P, H1], BF16, name="w1u_sb")
             bias_rows = setup.tile([P, P], F32, name="bias_rows")
             ident_f32 = setup.tile([P, P], F32, name="ident_f32")
-            zeros = setup.tile([P, BANK], BF16, name="zeros")
-            h_ps = setup_psum.tile([P, BANK], F32, name="h_ps")
-
-            nc.vector.memset(zeros[:], 0.0)
-            for i in range(WARM_MATMULS):
-                nc.tensor.matmul(h_ps[:], zeros[:, 0:P], zeros[:], start=True, stop=True)
 
             nc.vector.memset(bias_rows[:], 0.0)
             make_identity(nc, ident[:])
@@ -76,8 +78,9 @@ def tile_modelncf_b_kernel(tc, item_emb, user_emb, w1i, w1u, b1, w2, b2, offs, o
                     nc.scalar.copy(pi_sb[:, m, :], pi_ps[:])
                 else:
                     nc.vector.tensor_copy(pi_sb[:, m, :], pi_ps[:])
-            nc.tensor.matmul(h_ps[:, 0:N], ident[:], table[:].indirect(offsets[:]), start=True, stop=True)
-            nc.vector.tensor_copy(h_sb[:], h_ps[:, 0:N])
+            h_ps = setup_psum.tile([P, N], F32, name="h_ps")
+            nc.tensor.matmul(h_ps[:], ident[:], table[:].indirect(offsets[:]), start=True, stop=True)
+            nc.vector.tensor_copy(h_sb[:], h_ps[:])
 
             bias_ps = setup_psum.tile([P, P], F32, name="bias_ps")
             nc.tensor.transpose(bias_ps[:], bias_rows[:], ident_f32[:])
@@ -93,6 +96,7 @@ def tile_modelncf_b_kernel(tc, item_emb, user_emb, w1i, w1u, b1, w2, b2, offs, o
             tc.tile_pool(name="staged", bufs=6) as staged,
             tc.psum_pool(name="acc_psum", bufs=8) as acc_psum,
         ):
+            waiting = []
             first_user = 0
             for users in STORE_USERS:
                 mlp_out = staged.tile([P, users * N], F32, name="mlp_out")
@@ -119,17 +123,14 @@ def tile_modelncf_b_kernel(tc, item_emb, user_emb, w1i, w1u, b1, w2, b2, offs, o
                             start=(m == 0),
                             stop=(m == HID_BLOCKS - 1),
                         )
-                    nc.scalar.activation(
-                        mlp_out[:, pair * BANK : (pair + 1) * BANK],
-                        acc[:],
-                        RELU,
-                        bias=bias_cols[:, HID_BLOCKS : HID_BLOCKS + 1],
-                    )
+                    waiting.append((acc, mlp_out, pair, users, first_user))
+                    if len(waiting) > EVICT_LAG:
+                        evict_and_store(nc, out, b2_col, waiting.pop(0))
                     for t in range(PAIR):
                         u = first_user + pair * PAIR + t
                         col = (pair * PAIR + t) * N
                         nc.vector.tensor_scalar(gmf_out[:, col : col + N], h_sb[:], user_sb[:, u : u + 1], None, MULT)
-                cols = slice(first_user * N, (first_user + users) * N)
-                nc.sync.dma_start(out[0:D, cols], gmf_out[:])
-                nc.sync.dma_start(out[D : D + H2, cols], mlp_out[:])
+                nc.sync.dma_start(out[0:D, first_user * N : (first_user + users) * N], gmf_out[:])
                 first_user += users
+            for job in waiting:
+                evict_and_store(nc, out, b2_col, job)

@@ -11,21 +11,12 @@ SONG_BLOCKS = S // P
 HID_BLOCKS = H1 // P
 BANK = 512
 PAIR = BANK // N
-CHUNK = 8
-STORE_USERS = [CHUNK] * (U // CHUNK - 1) + [4, 2, 2]
+CHUNK = 4
 SCALAR_BLOCK = HID_BLOCKS - 1
 SHARED_BLOCK = HID_BLOCKS - 2
 SHARED_EVERY = 8
-EVICT_LAG = 2
 
 FLOPS = 2 * D * H1 * (N + U) + 2 * H1 * H2 * U * N
-
-
-def evict_and_store(nc, out, b2_col, job):
-    acc, mlp_out, pair, users, first_user = job
-    nc.scalar.activation(mlp_out[:, pair * BANK : (pair + 1) * BANK], acc[:], RELU, bias=b2_col)
-    if pair == users // PAIR - 1:
-        nc.sync.dma_start(out[D : D + H2, first_user * N : (first_user + users) * N], mlp_out[:])
 
 
 def tile_modelncf_b_kernel(tc, item_emb, user_emb, w1i, w1u, b1, w2, b2, offs, out):
@@ -40,7 +31,6 @@ def tile_modelncf_b_kernel(tc, item_emb, user_emb, w1i, w1u, b1, w2, b2, offs, o
         pi_sb = held.tile([P, HID_BLOCKS, N], F32, name="pi_sb")
         pub_sb = held.tile([P, HID_BLOCKS, U], F32, name="pub_sb")
         h_sb = held.tile([P, N], F32, name="h_sb")
-        b2_col = bias_cols[:, HID_BLOCKS : HID_BLOCKS + 1]
 
         with (
             tc.tile_pool(name="setup", bufs=1) as setup,
@@ -92,17 +82,15 @@ def tile_modelncf_b_kernel(tc, item_emb, user_emb, w1i, w1u, b1, w2, b2, offs, o
                 nc.vector.tensor_scalar(pub_sb[:, m, :], pu_ps[:, m, :], bias_cols[:, m : m + 1], None, ADD)
 
         with (
-            tc.tile_pool(name="hidden", bufs=3) as hidden,
-            tc.tile_pool(name="staged", bufs=6) as staged,
+            tc.tile_pool(name="hidden", bufs=6) as hidden,
+            tc.tile_pool(name="staged", bufs=8) as staged,
             tc.psum_pool(name="acc_psum", bufs=8) as acc_psum,
         ):
-            waiting = []
-            first_user = 0
-            for users in STORE_USERS:
-                mlp_out = staged.tile([P, users * N], F32, name="mlp_out")
-                gmf_out = staged.tile([P, users * N], F32, name="gmf_out")
-                h1 = hidden.tile([P, HID_BLOCKS, users * N], BF16, name="h1")
-                for pair in range(users // PAIR):
+            for first_user in range(0, U, CHUNK):
+                mlp_out = staged.tile([P, CHUNK * N], F32, name="mlp_out")
+                gmf_out = staged.tile([P, CHUNK * N], F32, name="gmf_out")
+                h1 = hidden.tile([P, HID_BLOCKS, CHUNK * N], BF16, name="h1")
+                for pair in range(CHUNK // PAIR):
                     for m in range(HID_BLOCKS):
                         for t in range(PAIR):
                             u = first_user + pair * PAIR + t
@@ -123,14 +111,16 @@ def tile_modelncf_b_kernel(tc, item_emb, user_emb, w1i, w1u, b1, w2, b2, offs, o
                             start=(m == 0),
                             stop=(m == HID_BLOCKS - 1),
                         )
-                    waiting.append((acc, mlp_out, pair, users, first_user))
-                    if len(waiting) > EVICT_LAG:
-                        evict_and_store(nc, out, b2_col, waiting.pop(0))
+                    nc.scalar.activation(
+                        mlp_out[:, pair * BANK : (pair + 1) * BANK],
+                        acc[:],
+                        RELU,
+                        bias=bias_cols[:, HID_BLOCKS : HID_BLOCKS + 1],
+                    )
                     for t in range(PAIR):
                         u = first_user + pair * PAIR + t
                         col = (pair * PAIR + t) * N
                         nc.vector.tensor_scalar(gmf_out[:, col : col + N], h_sb[:], user_sb[:, u : u + 1], None, MULT)
-                nc.sync.dma_start(out[0:D, first_user * N : (first_user + users) * N], gmf_out[:])
-                first_user += users
-            for job in waiting:
-                evict_and_store(nc, out, b2_col, job)
+                cols = slice(first_user * N, (first_user + CHUNK) * N)
+                nc.sync.dma_start(out[0:D, cols], gmf_out[:])
+                nc.sync.dma_start(out[D : D + H2, cols], mlp_out[:])

@@ -3,7 +3,7 @@ from concourse.masks import make_identity
 
 BF16, F32, U16 = mybir.dt.bfloat16, mybir.dt.float32, mybir.dt.uint16
 ADD, MAX, MULT = mybir.AluOpType.add, mybir.AluOpType.max, mybir.AluOpType.mult
-RELU = mybir.ActivationFunctionType.Relu
+RELU, IDENTITY = mybir.ActivationFunctionType.Relu, mybir.ActivationFunctionType.Identity
 
 P = 128
 S, D, U, N, H1, H2 = 512, 128, 128, 256, 512, 128
@@ -27,7 +27,8 @@ def tile_modelncf_b_kernel(tc, item_emb, user_emb, w1i, w1u, b1, w2, b2, offs, o
         ident = held.tile([P, P], BF16, name="ident")
         user_sb = held.tile([P, U], BF16, name="user_sb")
         w2_sb = held.tile([P, HID_BLOCKS, H2], BF16, name="w2_sb")
-        bias_cols = held.tile([P, HID_BLOCKS + 1], F32, name="bias_cols")
+        b1_cols = held.tile([P, HID_BLOCKS], F32, name="b1_cols")
+        b2_col = held.tile([P, 1], F32, name="b2_col")
         pi_sb = held.tile([P, HID_BLOCKS, N], F32, name="pi_sb")
         pub_sb = held.tile([P, HID_BLOCKS, U], F32, name="pub_sb")
         h_sb = held.tile([P, N], F32, name="h_sb")
@@ -39,25 +40,26 @@ def tile_modelncf_b_kernel(tc, item_emb, user_emb, w1i, w1u, b1, w2, b2, offs, o
             item_rows = setup.tile([P, SONG_BLOCKS, D], BF16, name="item_rows")
             w1i_sb = setup.tile([P, H1], BF16, name="w1i_sb")
             w1u_sb = setup.tile([P, H1], BF16, name="w1u_sb")
-            bias_rows = setup.tile([P, P], F32, name="bias_rows")
-            ident_f32 = setup.tile([P, P], F32, name="ident_f32")
-
-            nc.vector.memset(bias_rows[:], 0.0)
             make_identity(nc, ident[:])
-            nc.vector.tensor_copy(ident_f32[:], ident[:])
             nc.sync.dma_start(item_rows[:], item_emb.rearrange("(k p) e -> p k e", p=P))
             nc.sync.dma_start(offsets[:], offs)
-            nc.sync.dma_start(bias_rows[0:HID_BLOCKS, :], b1.rearrange("(k m) o -> k (m o)", m=P))
-            nc.sync.dma_start(bias_rows[HID_BLOCKS : HID_BLOCKS + 1, :], b2.rearrange("r o -> o r"))
+            nc.sync.dma_start(w1u_sb[:], w1u)
+            nc.sync.dma_start(user_sb[:], user_emb)
+            nc.sync.dma_start(w1i_sb[:], w1i)
+            nc.sync.dma_start(b1_cols[:], b1.rearrange("(k p) o -> p (k o)", p=P))
             nc.sync.dma_start(w2_sb[:], w2.rearrange("(k p) r -> p k r", p=P))
-            nc.scalar.dma_start(w1i_sb[:], w1i)
-            nc.scalar.dma_start(user_sb[:], user_emb)
-            nc.scalar.dma_start(w1u_sb[:], w1u)
+            nc.sync.dma_start(b2_col[:], b2)
 
             table_ps = setup_psum.tile([P, S], BF16, name="table_ps")
             for k in range(SONG_BLOCKS):
                 nc.tensor.transpose(table_ps[:, k * P : (k + 1) * P], item_rows[:, k, :], ident[:])
             nc.vector.tensor_copy(table[:], table_ps[:])
+
+            pu_ps = setup_psum.tile([P, HID_BLOCKS, U], F32, name="pu_ps")
+            for m in range(HID_BLOCKS):
+                nc.tensor.matmul(pu_ps[:, m, :], w1u_sb[:, m * P : (m + 1) * P], user_sb[:], start=True, stop=True)
+            for m in range(HID_BLOCKS):
+                nc.scalar.activation(pub_sb[:, m, :], pu_ps[:, m, :], IDENTITY, bias=b1_cols[:, m : m + 1])
 
             for m in range(HID_BLOCKS):
                 pi_ps = setup_psum.tile([P, N], F32, name=f"pi_ps{m}")
@@ -71,15 +73,6 @@ def tile_modelncf_b_kernel(tc, item_emb, user_emb, w1i, w1u, b1, w2, b2, offs, o
             h_ps = setup_psum.tile([P, N], F32, name="h_ps")
             nc.tensor.matmul(h_ps[:], ident[:], table[:].indirect(offsets[:]), start=True, stop=True)
             nc.vector.tensor_copy(h_sb[:], h_ps[:])
-
-            bias_ps = setup_psum.tile([P, P], F32, name="bias_ps")
-            nc.tensor.transpose(bias_ps[:], bias_rows[:], ident_f32[:])
-            nc.vector.tensor_copy(bias_cols[:], bias_ps[:, 0 : HID_BLOCKS + 1])
-
-            pu_ps = setup_psum.tile([P, HID_BLOCKS, U], F32, name="pu_ps")
-            for m in range(HID_BLOCKS):
-                nc.tensor.matmul(pu_ps[:, m, :], w1u_sb[:, m * P : (m + 1) * P], user_sb[:], start=True, stop=True)
-                nc.vector.tensor_scalar(pub_sb[:, m, :], pu_ps[:, m, :], bias_cols[:, m : m + 1], None, ADD)
 
         with (
             tc.tile_pool(name="hidden", bufs=6) as hidden,
@@ -115,7 +108,7 @@ def tile_modelncf_b_kernel(tc, item_emb, user_emb, w1i, w1u, b1, w2, b2, offs, o
                         mlp_out[:, pair * BANK : (pair + 1) * BANK],
                         acc[:],
                         RELU,
-                        bias=bias_cols[:, HID_BLOCKS : HID_BLOCKS + 1],
+                        bias=b2_col[:, 0:1],
                     )
                     for t in range(PAIR):
                         u = first_user + pair * PAIR + t

@@ -66,13 +66,10 @@ def tile_modelncf_b_kernel(tc, item_emb, user_emb, w1i, w1u, b1, w2, b2, offs, o
                 nc.tensor.matmul(
                     pi_ps[:], w1i_sb[:, m * P : (m + 1) * P], table[:].indirect(offsets[:]), start=True, stop=True
                 )
-                if m == SCALAR_BLOCK:
-                    nc.scalar.copy(pi_sb[:, m, :], pi_ps[:])
-                else:
-                    nc.vector.tensor_copy(pi_sb[:, m, :], pi_ps[:])
+                nc.scalar.copy(pi_sb[:, m, :], pi_ps[:])
             h_ps = setup_psum.tile([P, N], F32, name="h_ps")
             nc.tensor.matmul(h_ps[:], ident[:], table[:].indirect(offsets[:]), start=True, stop=True)
-            nc.vector.tensor_copy(h_sb[:], h_ps[:])
+            nc.scalar.copy(h_sb[:], h_ps[:])
 
         with (
             tc.tile_pool(name="hidden", bufs=6) as hidden,

@@ -40,6 +40,10 @@ def tile_modelncf_b_kernel(tc, item_emb, user_emb, w1i, w1u, b1, w2, b2, offs, o
             item_rows = setup.tile([P, SONG_BLOCKS, D], BF16, name="item_rows")
             w1i_sb = setup.tile([P, H1], BF16, name="w1i_sb")
             w1u_sb = setup.tile([P, H1], BF16, name="w1u_sb")
+            warm = setup.tile([P, 2], F32, name="warm")
+            nc.vector.memset(warm[:, 0:1], 0.0)
+            nc.scalar.activation(warm[:, 1:2], warm[:, 0:1], RELU)
+
             make_identity(nc, ident[:])
             nc.sync.dma_start(item_rows[:], item_emb.rearrange("(k p) e -> p k e", p=P))
             nc.sync.dma_start(offsets[:], offs)

import concourse.mybir as mybir
from concourse.masks import make_identity

BF16, F32, U16 = mybir.dt.bfloat16, mybir.dt.float32, mybir.dt.uint16
ADD, MAX, MULT = mybir.AluOpType.add, mybir.AluOpType.max, mybir.AluOpType.mult
RELU, IDENTITY = mybir.ActivationFunctionType.Relu, mybir.ActivationFunctionType.Identity

P = 128
S, D, U, N, H1, H2 = 512, 128, 128, 256, 512, 128
SONG_BLOCKS = S // P
HID_BLOCKS = H1 // P
BANK = 512
PAIR = BANK // N
CHUNK = 4
SCALAR_BLOCK = HID_BLOCKS - 1
SHARED_BLOCK = HID_BLOCKS - 2
SHARED_EVERY = 8

FLOPS = 2 * D * H1 * (N + U) + 2 * H1 * H2 * U * N


def tile_modelncf_b_kernel(tc, item_emb, user_emb, w1i, w1u, b1, w2, b2, offs, out):
    nc = tc.nc
    with tc.tile_pool(name="held", bufs=1) as held:
        offsets = held.tile([P, N // 16], U16, name="offsets")
        table = held.tile([P, S], BF16, name="table")
        ident = held.tile([P, P], BF16, name="ident")
        user_sb = held.tile([P, U], BF16, name="user_sb")
        w2_sb = held.tile([P, HID_BLOCKS, H2], BF16, name="w2_sb")
        b1_cols = held.tile([P, HID_BLOCKS], F32, name="b1_cols")
        b2_col = held.tile([P, 1], F32, name="b2_col")
        pi_sb = held.tile([P, HID_BLOCKS, N], F32, name="pi_sb")
        pub_sb = held.tile([P, HID_BLOCKS, U], F32, name="pub_sb")
        h_sb = held.tile([P, N], F32, name="h_sb")

        with (
            tc.tile_pool(name="setup", bufs=1) as setup,
            tc.psum_pool(name="setup_psum", bufs=1) as setup_psum,
        ):
            item_rows = setup.tile([P, SONG_BLOCKS, D], BF16, name="item_rows")
            w1i_sb = setup.tile([P, H1], BF16, name="w1i_sb")
            w1u_sb = setup.tile([P, H1], BF16, name="w1u_sb")
            warm = setup.tile([P, 2], F32, name="warm")
            nc.vector.memset(warm[:, 0:1], 0.0)
            nc.scalar.activation(warm[:, 1:2], warm[:, 0:1], RELU)

            make_identity(nc, ident[:])
            nc.sync.dma_start(item_rows[:], item_emb.rearrange("(k p) e -> p k e", p=P))
            nc.sync.dma_start(offsets[:], offs)
            nc.sync.dma_start(w1u_sb[:], w1u)
            nc.sync.dma_start(user_sb[:], user_emb)
            nc.sync.dma_start(w1i_sb[:], w1i)
            nc.sync.dma_start(b1_cols[:], b1.rearrange("(k p) o -> p (k o)", p=P))
            nc.sync.dma_start(w2_sb[:], w2.rearrange("(k p) r -> p k r", p=P))
            nc.sync.dma_start(b2_col[:], b2)

            table_ps = setup_psum.tile([P, S], BF16, name="table_ps")
            for k in range(SONG_BLOCKS):
                nc.tensor.transpose(table_ps[:, k * P : (k + 1) * P], item_rows[:, k, :], ident[:])
            nc.vector.tensor_copy(table[:], table_ps[:])

            pu_ps = setup_psum.tile([P, HID_BLOCKS, U], F32, name="pu_ps")
            for m in range(HID_BLOCKS):
                nc.tensor.matmul(pu_ps[:, m, :], w1u_sb[:, m * P : (m + 1) * P], user_sb[:], start=True, stop=True)
            for m in range(HID_BLOCKS):
                nc.scalar.activation(pub_sb[:, m, :], pu_ps[:, m, :], IDENTITY, bias=b1_cols[:, m : m + 1])

            for m in range(HID_BLOCKS):
                pi_ps = setup_psum.tile([P, N], F32, name=f"pi_ps{m}")
                nc.tensor.matmul(
                    pi_ps[:], w1i_sb[:, m * P : (m + 1) * P], table[:].indirect(offsets[:]), start=True, stop=True
                )
                nc.scalar.copy(pi_sb[:, m, :], pi_ps[:])
            h_ps = setup_psum.tile([P, N], F32, name="h_ps")
            nc.tensor.matmul(h_ps[:], ident[:], table[:].indirect(offsets[:]), start=True, stop=True)
            nc.scalar.copy(h_sb[:], h_ps[:])

        with (
            tc.tile_pool(name="hidden", bufs=6) as hidden,
            tc.tile_pool(name="staged", bufs=8) as staged,
            tc.psum_pool(name="acc_psum", bufs=8) as acc_psum,
        ):
            for first_user in range(0, U, CHUNK):
                mlp_out = staged.tile([P, CHUNK * N], F32, name="mlp_out")
                gmf_out = staged.tile([P, CHUNK * N], F32, name="gmf_out")
                h1 = hidden.tile([P, HID_BLOCKS, CHUNK * N], BF16, name="h1")
                for pair in range(CHUNK // PAIR):
                    for m in range(HID_BLOCKS):
                        for t in range(PAIR):
                            u = first_user + pair * PAIR + t
                            col = (pair * PAIR + t) * N
                            h1_piece = h1[:, m, col : col + N]
                            if m == SCALAR_BLOCK or (m == SHARED_BLOCK and u % SHARED_EVERY == SHARED_EVERY - 1):
                                nc.scalar.activation(h1_piece, pi_sb[:, m, :], RELU, bias=pub_sb[:, m, u : u + 1])
                            else:
                                nc.vector.tensor_scalar(
                                    h1_piece, pi_sb[:, m, :], pub_sb[:, m, u : u + 1], 0.0, ADD, MAX
                                )
                    acc = acc_psum.tile([P, BANK], F32, name="acc")
                    for m in range(HID_BLOCKS):
                        nc.tensor.matmul(
                            acc[:],
                            w2_sb[:, m, :],
                            h1[:, m, pair * BANK : (pair + 1) * BANK],
                            start=(m == 0),
                            stop=(m == HID_BLOCKS - 1),
                        )
                    nc.scalar.activation(
                        mlp_out[:, pair * BANK : (pair + 1) * BANK],
                        acc[:],
                        RELU,
                        bias=b2_col[:, 0:1],
                    )
                    for t in range(PAIR):
                        u = first_user + pair * PAIR + t
                        col = (pair * PAIR + t) * N
                        nc.vector.tensor_scalar(gmf_out[:, col : col + N], h_sb[:], user_sb[:, u : u + 1], None, MULT)
                cols = slice(first_user * N, (first_user + CHUNK) * N)
                nc.sync.dma_start(out[0:D, cols], gmf_out[:])
                nc.sync.dma_start(out[D : D + H2, cols], mlp_out[:])
